import numpy as np
import ml_dtypes


def mxq(x, axis, fmt="e4m3"):
    dtype, down = {"e4m3": (ml_dtypes.float8_e4m3fn, 7), "e5m2": (ml_dtypes.float8_e5m2, 14)}[fmt]
    v = np.moveaxis(np.asarray(x, np.float32).astype(ml_dtypes.bfloat16).astype(np.float64), axis, -1)
    blocks = v.reshape(v.shape[:-1] + (-1, 32))
    amax = np.abs(blocks).max(-1, keepdims=True)
    byte = np.maximum(np.where(amax > 0, np.frexp(amax)[1] - 1 + 127, 0) - down, 1)
    scale = np.exp2(byte - 127.0)
    codes = (blocks / scale).astype(np.float32).astype(dtype).astype(np.float64)
    return np.moveaxis((codes * scale).reshape(v.shape), -1, axis)


WIDE = False


def mx_kscale(k):
    if not WIDE:
        return np.ones(k)
    levels = np.array([10, -10, 5, -5, 0])
    a = np.random.permutation(np.resize(levels, k // 512 * 4)).reshape(k // 512, 4)
    idx = np.arange(k)
    return np.exp2(a[idx // 512, idx % 128 // 32])


BF16 = ml_dtypes.bfloat16


def bf(x):
    return np.asarray(x, np.float32).astype(BF16)


def f64(x):
    return np.asarray(x).astype(np.float64)


B, Q, K, D = 8, 1024, 512, 512
NEG = -10000.0


def setup_inputs():
    s, t = mx_kscale(D), mx_kscale(D)
    return {"query": bf(np.random.standard_normal((B, Q, D)) * s),
            "context": bf(np.random.standard_normal((B, K, D)) * 0.5 / t),
            "query_bit": bf(np.random.random((B, Q)) > 0.25),
            "context_bit": bf(np.random.random((B, K)) > 0.25),
            "W_in": bf(np.random.standard_normal((D, D)) * 4.0 / D * t[:, None] / s[None, :]),
            "b_in": bf(np.random.standard_normal(D) / np.sqrt(D) * t)}


def reference(query, context, query_bit, context_bit, W_in, b_in):
    ext = (1.0 - f64(query_bit)[:, :, None] * f64(context_bit)[:, None, :]) * NEG
    q = (mxq(f64(query), 2, "e4m3") @ mxq(f64(W_in), 1, "e4m3").T) + f64(b_in)
    scores = (mxq(q, 2, "e4m3") @ mxq(f64(context), 2, "e4m3").transpose(0, 2, 1)) + ext
    e = np.exp(scores - scores.max(-1, keepdims=True))
    return e / e.sum(-1, keepdims=True)

@@ -1,0 +1,216 @@
+from contextlib import ExitStack
+
+import concourse.bass as bass
+import concourse.mybir as mybir
+import concourse.tile as tile
+from concourse.masks import make_identity
+
+F32 = mybir.dt.float32
+BF16 = mybir.dt.bfloat16
+U32 = mybir.dt.uint32
+U8 = mybir.dt.uint8
+FP8X4 = mybir.dt.float8_e4m3fn_x4
+ALU = mybir.AluOpType
+ACT = mybir.ActivationFunctionType
+AX = mybir.AxisListType
+
+P = 128
+B, Q, K, D = 8, 1024, 512, 512
+FLOPS = 2 * (2 * B * Q * D * D)
+UNITS = 2 * B
+
+
+def tile_attention_pa_t_kernel(tc, query, context, query_bit, context_bit, W_in, b_in, out):
+    nc = tc.nc
+    with ExitStack() as ctx:
+        const = ctx.enter_context(tc.tile_pool(name="const", bufs=1))
+        xin = ctx.enter_context(tc.tile_pool(name="xin", bufs=3))
+        work = ctx.enter_context(tc.tile_pool(name="work", bufs=2))
+        soft = ctx.enter_context(tc.tile_pool(name="soft", bufs=4))
+        ps_t = ctx.enter_context(tc.psum_pool(name="ps_t", bufs=2))
+        ps_q = ctx.enter_context(tc.psum_pool(name="ps_q", bufs=3))
+        ps_s = ctx.enter_context(tc.psum_pool(name="ps_s", bufs=3))
+
+        W_sb = const.tile([P, 4, D], BF16, name="W_sb")
+        nc.sync.dma_start(
+            out=W_sb[:].rearrange("m (u e) k -> m u (e k)", u=2),
+            in_=W_in.rearrange("(u m e) k -> m u (e k)", u=2, e=2),
+        )
+        x_tiles = {}
+        c_tiles = {}
+
+        def load(b):
+            x_sb = xin.tile([P, 8, D], BF16, name="x_sb")
+            nc.sync.dma_start(out=x_sb[:], in_=query[b].rearrange("(p t) k -> p t k", t=8))
+            c_sb = xin.tile([P, 4, D], BF16, name="c_sb")
+            nc.sync.dma_start(out=c_sb[:], in_=context[b].rearrange("(t p) k -> p t k", p=P))
+            x_tiles[b] = x_sb
+            c_tiles[b] = c_sb
+
+        load(0)
+        load(1)
+
+        ident = const.tile([P, P], F32, name="ident")
+        make_identity(nc, ident[:])
+
+        b_bf = const.tile([P, 4], BF16, name="b_bf")
+        qb_bf = const.tile([P, B, 8], BF16, name="qb_bf")
+        with nc.allow_non_contiguous_dma(reason="two small vectors, loaded once"):
+            nc.scalar.dma_start(
+                out=b_bf[:].rearrange("m (u e) -> m u e", u=2),
+                in_=b_in.rearrange("(u m e) -> m u e", u=2, e=2),
+            )
+            nc.scalar.dma_start(out=qb_bf[:], in_=query_bit.rearrange("b (p t) -> p b t", t=8))
+        cb_all = const.tile([P, B * K], BF16, name="cb_all")
+        nc.scalar.dma_start(out=cb_all[:], in_=context_bit.rearrange("b j -> (b j)").partition_broadcast(P))
+
+        b_f = const.tile([P, 4], F32, name="b_f")
+        nc.vector.tensor_copy(out=b_f[:], in_=b_bf[:])
+        pa = const.tile([P, B * 8], F32, name="pa")
+        nc.vector.tensor_scalar(
+            out=pa[:], in0=qb_bf[:].rearrange("p b t -> p (b t)"), scalar1=10000.0, scalar2=None, op0=ALU.mult
+        )
+        dead = const.tile([P, B * K], BF16, name="dead")
+        nc.vector.tensor_scalar(
+            out=dead[:], in0=cb_all[:], scalar1=-1.0, scalar2=1.0, op0=ALU.mult, op1=ALU.add
+        )
+
+        def transpose_group(src_f32, n_tiles, grouped_f32):
+            for h in range(n_tiles // 2):
+                tp = ps_t.tile([P, 4, P], F32, name="tp")
+                for a in range(2):
+                    for u in range(2):
+                        nc.tensor.transpose(
+                            tp[:, 2 * a + u, :], src_f32[:, 2 * h + a, P * u : P * (u + 1)], ident[:]
+                        )
+                nc.scalar.copy(
+                    out=grouped_f32[:, 2 * h : 2 * h + 2, :, :],
+                    in_=tp[:].rearrange("p (a u) m -> p a m u", a=2),
+                )
+
+        Wg = const.tile([P, 4, P, 4], BF16, name="Wg", align_bytes=64)
+        Wc = const.tile([P, 4 * P], U32, name="Wc", align_bytes=64)
+        Ws = const.tile([P, 4 * P], U8, name="Ws", align_bytes=64)
+        transpose_group(W_sb[:].bitcast(F32), 4, Wg[:].bitcast(F32))
+        nc.vector.quantize_mx(
+            out=Wc[:].bitcast(FP8X4), scales=Ws[:], in_=Wg[:].rearrange("p t m v -> p (t m v)")
+        )
+
+        ctx_q = {}
+        x_q = {}
+        q_q = {}
+
+        def stage_ctx(b):
+            cg = work.tile([P, 4, P, 4], BF16, name="cg", align_bytes=64)
+            cc = work.tile([P, K], U32, name="cc", align_bytes=64)
+            cs = work.tile([P, K], U8, name="cs", align_bytes=64)
+            transpose_group(c_tiles[b][:].bitcast(F32), 4, cg[:].bitcast(F32))
+            nc.vector.quantize_mx(
+                out=cc[:].bitcast(FP8X4), scales=cs[:], in_=cg[:].rearrange("p t m v -> p (t m v)")
+            )
+            ctx_q[b] = (cc, cs)
+
+        def stage_x(n):
+            b, h = n // 2, n % 2
+            xg = work.tile([P, 4, P, 4], BF16, name="xg", align_bytes=64)
+            xc = work.tile([P, 512], U32, name="xc", align_bytes=64)
+            xs = work.tile([P, 512], U8, name="xs", align_bytes=64)
+            transpose_group(x_tiles[b][:, 4 * h : 4 * h + 4, :].bitcast(F32), 4, xg[:].bitcast(F32))
+            nc.vector.quantize_mx(
+                out=xc[:].bitcast(FP8X4), scales=xs[:], in_=xg[:].rearrange("p t m v -> p (t m v)")
+            )
+            x_q[n] = (xc, xs)
+
+        def stage_q(n):
+            xc, xs = x_q[n]
+            q_bf = work.tile([P, 4, 512], BF16, name="q_bf")
+            for t in range(4):
+                qp = ps_q.tile([P, 512], F32, name="qp")
+                nc.tensor.matmul_mx(
+                    out=qp[:],
+                    lhsT=Wc[:, P * t : P * (t + 1)].bitcast(FP8X4),
+                    lhsT_scale=Ws[:, P * t : P * (t + 1)],
+                    rhs=xc[:].bitcast(FP8X4),
+                    rhs_scale=xs[:],
+                    start=True,
+                    stop=True,
+                )
+                nc.scalar.activation(
+                    out=q_bf[:, t, :], in_=qp[:], func=ACT.Identity, bias=b_f[:, t : t + 1], scale=1.0
+                )
+            qg = work.tile([P, 512, 4], BF16, name="qg", align_bytes=64)
+            qc = work.tile([P, 512], U32, name="qc", align_bytes=64)
+            qs = work.tile([P, 512], U8, name="qs", align_bytes=64)
+            nc.vector.tensor_copy(
+                out=qg[:].rearrange("p (c i) t -> p c t i", i=4),
+                in_=q_bf[:].rearrange("p t (c i) -> p c t i", i=4),
+            )
+            nc.vector.quantize_mx(
+                out=qc[:].bitcast(FP8X4), scales=qs[:], in_=qg[:].rearrange("p c t -> p (c t)")
+            )
+            q_q[n] = (qc, qs)
+
+        def stage_s(n):
+            b, h = n // 2, n % 2
+            qc, qs = q_q[n]
+            cc, cs = ctx_q[b]
+            z = soft.tile([P, 4, K], F32, name="z")
+            nm = soft.tile([P, 4], F32, name="nm")
+            ssum = soft.tile([P, 4], F32, name="ssum")
+            r = soft.tile([P, 4], F32, name="r")
+            for k in range(4):
+                sp = ps_s.tile([P, K], F32, name="sp")
+                nc.tensor.matmul_mx(
+                    out=sp[:],
+                    lhsT=qc[:, P * k : P * (k + 1)].bitcast(FP8X4),
+                    lhsT_scale=qs[:, P * k : P * (k + 1)],
+                    rhs=cc[:].bitcast(FP8X4),
+                    rhs_scale=cs[:],
+                    start=True,
+                    stop=True,
+                )
+                col = 8 * b + 4 * h + k
+                nc.vector.scalar_tensor_tensor(
+                    out=z[:, k, :],
+                    in0=dead[:, K * b : K * (b + 1)],
+                    scalar=pa[:, col : col + 1],
+                    in1=sp[:],
+                    op0=ALU.mult,
+                    op1=ALU.subtract,
+                )
+            nc.vector.tensor_reduce(out=nm[:], in_=z[:], axis=AX.X, op=ALU.min)
+            for k in range(4):
+                nc.scalar.activation(
+                    out=z[:, k, :],
+                    in_=z[:, k, :],
+                    func=ACT.Exp,
+                    bias=nm[:, k : k + 1],
+                    scale=-1.0,
+                    accum_out=ssum[:, k : k + 1],
+                )
+            nc.vector.reciprocal(out=r[:], in_=ssum[:])
+            for k in range(4):
+                nc.gpsimd.tensor_scalar(
+                    out=z[:, k, :],
+                    in0=z[:, k, :],
+                    scalar1=r[:, k : k + 1],
+                    scalar2=0.0,
+                    op0=ALU.mult,
+                    op1=ALU.add,
+                )
+            nc.sync.dma_start(
+                out=out[b].rearrange("(p t) j -> p t j", t=8)[:, 4 * h : 4 * h + 4, :], in_=z[:]
+            )
+
+        for n in range(UNITS + 2):
+            if n < UNITS:
+                b, h = n // 2, n % 2
+                if h == 0:
+                    if b + 2 < B:
+                        load(b + 2)
+                    stage_ctx(b)
+                stage_x(n)
+            if 1 <= n <= UNITS:
+                stage_q(n - 1)
+            if n >= 2:
+                stage_s(n - 2)

@@ -1,8 +1,6 @@
 from contextlib import ExitStack
 
-import concourse.bass as bass
 import concourse.mybir as mybir
-import concourse.tile as tile
 from concourse.masks import make_identity
 
 F32 = mybir.dt.float32
@@ -23,30 +21,40 @@ UNITS = 2 * B
 def tile_attention_pa_t_kernel(tc, query, context, query_bit, context_bit, W_in, b_in, out):
     nc = tc.nc
     with ExitStack() as ctx:
+        ctx.enter_context(tc.manual_schedule())
         const = ctx.enter_context(tc.tile_pool(name="const", bufs=1))
-        xin = ctx.enter_context(tc.tile_pool(name="xin", bufs=3))
+        xin = ctx.enter_context(tc.tile_pool(name="xin", bufs=4))
+        cin = ctx.enter_context(tc.tile_pool(name="cin", bufs=2))
         work = ctx.enter_context(tc.tile_pool(name="work", bufs=2))
+        keep = ctx.enter_context(tc.tile_pool(name="keep", bufs=3))
         soft = ctx.enter_context(tc.tile_pool(name="soft", bufs=4))
         ps_t = ctx.enter_context(tc.psum_pool(name="ps_t", bufs=2))
-        ps_q = ctx.enter_context(tc.psum_pool(name="ps_q", bufs=3))
-        ps_s = ctx.enter_context(tc.psum_pool(name="ps_s", bufs=3))
+        ps_q = ctx.enter_context(tc.psum_pool(name="ps_q", bufs=2))
+        ps_s = ctx.enter_context(tc.psum_pool(name="ps_s", bufs=4))
+
+        x_in, c_in, x_grp, c_grp, x_mx, c_mx = {}, {}, {}, {}, {}, {}
+        q_rows, q_grp, q_mx, s_ps, z_of, nm_of, sum_of = {}, {}, {}, {}, {}, {}, {}
+
+        def unit(n):
+            return 0 <= n < UNITS
+
+        def load(n):
+            b, h = n // 2, n % 2
+            x_sb = xin.tile([P, 4, D], BF16, name="x_sb")
+            nc.sync.dma_start(
+                out=x_sb[:], in_=query[b].rearrange("(p t) k -> p t k", t=8)[:, 4 * h : 4 * h + 4, :]
+            )
+            x_in[n] = x_sb
+            if h == 0:
+                c_sb = cin.tile([P, 4, D], BF16, name="c_sb")
+                nc.sync.dma_start(out=c_sb[:], in_=context[b].rearrange("(t p) k -> p t k", p=P))
+                c_in[b] = c_sb
 
         W_sb = const.tile([P, 4, D], BF16, name="W_sb")
         nc.sync.dma_start(
             out=W_sb[:].rearrange("m (u e) k -> m u (e k)", u=2),
             in_=W_in.rearrange("(u m e) k -> m u (e k)", u=2, e=2),
         )
-        x_tiles = {}
-        c_tiles = {}
-
-        def load(b):
-            x_sb = xin.tile([P, 8, D], BF16, name="x_sb")
-            nc.sync.dma_start(out=x_sb[:], in_=query[b].rearrange("(p t) k -> p t k", t=8))
-            c_sb = xin.tile([P, 4, D], BF16, name="c_sb")
-            nc.sync.dma_start(out=c_sb[:], in_=context[b].rearrange("(t p) k -> p t k", p=P))
-            x_tiles[b] = x_sb
-            c_tiles[b] = c_sb
-
         load(0)
         load(1)
 
@@ -71,12 +79,9 @@ def tile_attention_pa_t_kernel(tc, query, context, query_bit, context_bit, W_in,
             out=pa[:], in0=qb_bf[:].rearrange("p b t -> p (b t)"), scalar1=10000.0, scalar2=None, op0=ALU.mult
         )
         dead = const.tile([P, B * K], BF16, name="dead")
-        nc.vector.tensor_scalar(
-            out=dead[:], in0=cb_all[:], scalar1=-1.0, scalar2=1.0, op0=ALU.mult, op1=ALU.add
-        )
 
-        def transpose_group(src_f32, n_tiles, grouped_f32):
-            for h in range(n_tiles // 2):
+        def transposes(src_f32, grouped_f32):
+            for h in range(2):
                 tp = ps_t.tile([P, 4, P], F32, name="tp")
                 for a in range(2):
                     for u in range(2):
@@ -88,41 +93,39 @@ def tile_attention_pa_t_kernel(tc, query, context, query_bit, context_bit, W_in,
                     in_=tp[:].rearrange("p (a u) m -> p a m u", a=2),
                 )
 
+        def quantise(grouped, codes, scales):
+            nc.vector.quantize_mx(
+                out=codes[:].bitcast(FP8X4), scales=scales[:], in_=grouped[:].rearrange("p t m v -> p (t m v)")
+            )
+
         Wg = const.tile([P, 4, P, 4], BF16, name="Wg", align_bytes=64)
         Wc = const.tile([P, 4 * P], U32, name="Wc", align_bytes=64)
         Ws = const.tile([P, 4 * P], U8, name="Ws", align_bytes=64)
-        transpose_group(W_sb[:].bitcast(F32), 4, Wg[:].bitcast(F32))
-        nc.vector.quantize_mx(
-            out=Wc[:].bitcast(FP8X4), scales=Ws[:], in_=Wg[:].rearrange("p t m v -> p (t m v)")
-        )
+        transposes(W_sb[:].bitcast(F32), Wg[:].bitcast(F32))
+        quantise(Wg, Wc, Ws)
 
-        ctx_q = {}
-        x_q = {}
-        q_q = {}
-
-        def stage_ctx(b):
-            cg = work.tile([P, 4, P, 4], BF16, name="cg", align_bytes=64)
-            cc = work.tile([P, K], U32, name="cc", align_bytes=64)
-            cs = work.tile([P, K], U8, name="cs", align_bytes=64)
-            transpose_group(c_tiles[b][:].bitcast(F32), 4, cg[:].bitcast(F32))
-            nc.vector.quantize_mx(
-                out=cc[:].bitcast(FP8X4), scales=cs[:], in_=cg[:].rearrange("p t m v -> p (t m v)")
-            )
-            ctx_q[b] = (cc, cs)
-
-        def stage_x(n):
-            b, h = n // 2, n % 2
+        def x_transpose(n):
             xg = work.tile([P, 4, P, 4], BF16, name="xg", align_bytes=64)
+            transposes(x_in[n][:].bitcast(F32), xg[:].bitcast(F32))
+            x_grp[n] = xg
+            if n % 2 == 0:
+                cg = work.tile([P, 4, P, 4], BF16, name="cg", align_bytes=64)
+                transposes(c_in[n // 2][:].bitcast(F32), cg[:].bitcast(F32))
+                c_grp[n // 2] = cg
+
+        def x_quantise(n):
             xc = work.tile([P, 512], U32, name="xc", align_bytes=64)
             xs = work.tile([P, 512], U8, name="xs", align_bytes=64)
-            transpose_group(x_tiles[b][:, 4 * h : 4 * h + 4, :].bitcast(F32), 4, xg[:].bitcast(F32))
-            nc.vector.quantize_mx(
-                out=xc[:].bitcast(FP8X4), scales=xs[:], in_=xg[:].rearrange("p t m v -> p (t m v)")
-            )
-            x_q[n] = (xc, xs)
+            quantise(x_grp[n], xc, xs)
+            x_mx[n] = (xc, xs)
+            if n % 2 == 0:
+                cc = keep.tile([P, K], U32, name="cc", align_bytes=64)
+                cs = keep.tile([P, K], U8, name="cs", align_bytes=64)
+                quantise(c_grp[n // 2], cc, cs)
+                c_mx[n // 2] = (cc, cs)
 
-        def stage_q(n):
-            xc, xs = x_q[n]
+        def q_matmuls(n):
+            xc, xs = x_mx[n]
             q_bf = work.tile([P, 4, 512], BF16, name="q_bf")
             for t in range(4):
                 qp = ps_q.tile([P, 512], F32, name="qp")
@@ -138,26 +141,28 @@ def tile_attention_pa_t_kernel(tc, query, context, query_bit, context_bit, W_in,
                 nc.scalar.activation(
                     out=q_bf[:, t, :], in_=qp[:], func=ACT.Identity, bias=b_f[:, t : t + 1], scale=1.0
                 )
+            q_rows[n] = q_bf
+
+        def q_regroup(n):
             qg = work.tile([P, 512, 4], BF16, name="qg", align_bytes=64)
-            qc = work.tile([P, 512], U32, name="qc", align_bytes=64)
-            qs = work.tile([P, 512], U8, name="qs", align_bytes=64)
             nc.vector.tensor_copy(
                 out=qg[:].rearrange("p (c i) t -> p c t i", i=4),
-                in_=q_bf[:].rearrange("p t (c i) -> p c t i", i=4),
+                in_=q_rows[n][:].rearrange("p t (c i) -> p c t i", i=4),
             )
-            nc.vector.quantize_mx(
-                out=qc[:].bitcast(FP8X4), scales=qs[:], in_=qg[:].rearrange("p c t -> p (c t)")
-            )
-            q_q[n] = (qc, qs)
+            q_grp[n] = qg
 
-        def stage_s(n):
-            b, h = n // 2, n % 2
-            qc, qs = q_q[n]
-            cc, cs = ctx_q[b]
-            z = soft.tile([P, 4, K], F32, name="z")
-            nm = soft.tile([P, 4], F32, name="nm")
-            ssum = soft.tile([P, 4], F32, name="ssum")
-            r = soft.tile([P, 4], F32, name="r")
+        def q_quantise(n):
+            qc = keep.tile([P, 512], U32, name="qc", align_bytes=64)
+            qs = keep.tile([P, 512], U8, name="qs", align_bytes=64)
+            nc.vector.quantize_mx(
+                out=qc[:].bitcast(FP8X4), scales=qs[:], in_=q_grp[n][:].rearrange("p c t -> p (c t)")
+            )
+            q_mx[n] = (qc, qs)
+
+        def s_matmuls(n):
+            qc, qs = q_mx[n]
+            cc, cs = c_mx[n // 2]
+            s_ps[n] = []
             for k in range(4):
                 sp = ps_s.tile([P, K], F32, name="sp")
                 nc.tensor.matmul_mx(
@@ -169,48 +174,92 @@ def tile_attention_pa_t_kernel(tc, query, context, query_bit, context_bit, W_in,
                     start=True,
                     stop=True,
                 )
-                col = 8 * b + 4 * h + k
+                s_ps[n].append(sp)
+
+        def normalise(n):
+            b, h = n // 2, n % 2
+            z = z_of[n]
+            rows = out[b].rearrange("(p t) j -> p t j", t=8)
+            r = soft.tile([P, 4], F32, name="r")
+            if n == UNITS - 1:
+                for k in range(4):
+                    nc.vector.reciprocal(out=r[:, k : k + 1], in_=sum_of[n][:, k : k + 1])
+                    nc.vector.tensor_scalar(
+                        out=z[:, k, :], in0=z[:, k, :], scalar1=r[:, k : k + 1], scalar2=None, op0=ALU.mult
+                    )
+                    nc.sync.dma_start(out=rows[:, 4 * h + k, :], in_=z[:, k, :])
+            else:
+                nc.vector.reciprocal(out=r[:], in_=sum_of[n][:])
+                for k in range(4):
+                    nc.gpsimd.tensor_scalar(
+                        out=z[:, k, :],
+                        in0=z[:, k, :],
+                        scalar1=r[:, k : k + 1],
+                        scalar2=0.0,
+                        op0=ALU.mult,
+                        op1=ALU.add,
+                    )
+                nc.sync.dma_start(out=rows[:, 4 * h : 4 * h + 4, :], in_=z[:])
+
+        def s_mask_min(n):
+            b = n // 2
+            z = soft.tile([P, 4, K], F32, name="z")
+            nm = soft.tile([P, 4], F32, name="nm")
+            z_of[n] = z
+            nm_of[n] = nm
+            for k in range(4):
+                col = 4 * n + k
                 nc.vector.scalar_tensor_tensor(
                     out=z[:, k, :],
                     in0=dead[:, K * b : K * (b + 1)],
                     scalar=pa[:, col : col + 1],
-                    in1=sp[:],
+                    in1=s_ps[n][k][:],
                     op0=ALU.mult,
                     op1=ALU.subtract,
                 )
-            nc.vector.tensor_reduce(out=nm[:], in_=z[:], axis=AX.X, op=ALU.min)
+                if k == 0 and unit(n - 1):
+                    normalise(n - 1)
+                if n == UNITS - 1:
+                    nc.vector.tensor_reduce(out=nm[:, k : k + 1], in_=z[:, k, :], axis=AX.X, op=ALU.min)
+            if n != UNITS - 1:
+                nc.vector.tensor_reduce(out=nm[:], in_=z[:], axis=AX.X, op=ALU.min)
+
+        def s_exp(n):
+            z = z_of[n]
+            ssum = soft.tile([P, 4], F32, name="ssum")
+            sum_of[n] = ssum
             for k in range(4):
                 nc.scalar.activation(
                     out=z[:, k, :],
                     in_=z[:, k, :],
                     func=ACT.Exp,
-                    bias=nm[:, k : k + 1],
+                    bias=nm_of[n][:, k : k + 1],
                     scale=-1.0,
                     accum_out=ssum[:, k : k + 1],
                 )
-            nc.vector.reciprocal(out=r[:], in_=ssum[:])
-            for k in range(4):
-                nc.gpsimd.tensor_scalar(
-                    out=z[:, k, :],
-                    in0=z[:, k, :],
-                    scalar1=r[:, k : k + 1],
-                    scalar2=0.0,
-                    op0=ALU.mult,
-                    op1=ALU.add,
-                )
-            nc.sync.dma_start(
-                out=out[b].rearrange("(p t) j -> p t j", t=8)[:, 4 * h : 4 * h + 4, :], in_=z[:]
-            )
 
-        for n in range(UNITS + 2):
-            if n < UNITS:
-                b, h = n // 2, n % 2
-                if h == 0:
-                    if b + 2 < B:
-                        load(b + 2)
-                    stage_ctx(b)
-                stage_x(n)
-            if 1 <= n <= UNITS:
-                stage_q(n - 1)
-            if n >= 2:
-                stage_s(n - 2)
+        for n in range(-3, UNITS + 1):
+            if unit(n + 5):
+                load(n + 5)
+            if n == 0:
+                nc.vector.tensor_scalar(
+                    out=dead[:], in0=cb_all[:], scalar1=-1.0, scalar2=1.0, op0=ALU.mult, op1=ALU.add
+                )
+            if unit(n):
+                s_mask_min(n)
+            if n == UNITS:
+                normalise(n - 1)
+            if unit(n + 2):
+                q_matmuls(n + 2)
+            if unit(n + 3):
+                x_transpose(n + 3)
+            if unit(n):
+                s_exp(n)
+            if unit(n + 1):
+                s_matmuls(n + 1)
+            if unit(n + 2):
+                q_regroup(n + 2)
+            if unit(n + 3):
+                x_quantise(n + 3)
+            if unit(n + 2):
+                q_quantise(n + 2)

@@ -1,6 +1,8 @@
 from contextlib import ExitStack
 
+import concourse.bass as bass
 import concourse.mybir as mybir
+import concourse.tile as tile
 from concourse.masks import make_identity
 
 F32 = mybir.dt.float32
@@ -21,40 +23,30 @@ UNITS = 2 * B
 def tile_attention_pa_t_kernel(tc, query, context, query_bit, context_bit, W_in, b_in, out):
     nc = tc.nc
     with ExitStack() as ctx:
-        ctx.enter_context(tc.manual_schedule())
         const = ctx.enter_context(tc.tile_pool(name="const", bufs=1))
-        xin = ctx.enter_context(tc.tile_pool(name="xin", bufs=4))
-        cin = ctx.enter_context(tc.tile_pool(name="cin", bufs=2))
+        xin = ctx.enter_context(tc.tile_pool(name="xin", bufs=3))
         work = ctx.enter_context(tc.tile_pool(name="work", bufs=2))
-        keep = ctx.enter_context(tc.tile_pool(name="keep", bufs=3))
         soft = ctx.enter_context(tc.tile_pool(name="soft", bufs=4))
         ps_t = ctx.enter_context(tc.psum_pool(name="ps_t", bufs=2))
-        ps_q = ctx.enter_context(tc.psum_pool(name="ps_q", bufs=2))
-        ps_s = ctx.enter_context(tc.psum_pool(name="ps_s", bufs=4))
-
-        x_in, c_in, x_grp, c_grp, x_mx, c_mx = {}, {}, {}, {}, {}, {}
-        q_rows, q_grp, q_mx, s_ps, z_of, nm_of, sum_of = {}, {}, {}, {}, {}, {}, {}
-
-        def unit(n):
-            return 0 <= n < UNITS
-
-        def load(n):
-            b, h = n // 2, n % 2
-            x_sb = xin.tile([P, 4, D], BF16, name="x_sb")
-            nc.sync.dma_start(
-                out=x_sb[:], in_=query[b].rearrange("(p t) k -> p t k", t=8)[:, 4 * h : 4 * h + 4, :]
-            )
-            x_in[n] = x_sb
-            if h == 0:
-                c_sb = cin.tile([P, 4, D], BF16, name="c_sb")
-                nc.sync.dma_start(out=c_sb[:], in_=context[b].rearrange("(t p) k -> p t k", p=P))
-                c_in[b] = c_sb
+        ps_q = ctx.enter_context(tc.psum_pool(name="ps_q", bufs=3))
+        ps_s = ctx.enter_context(tc.psum_pool(name="ps_s", bufs=3))
 
         W_sb = const.tile([P, 4, D], BF16, name="W_sb")
         nc.sync.dma_start(
             out=W_sb[:].rearrange("m (u e) k -> m u (e k)", u=2),
             in_=W_in.rearrange("(u m e) k -> m u (e k)", u=2, e=2),
         )
+        x_tiles = {}
+        c_tiles = {}
+
+        def load(b):
+            x_sb = xin.tile([P, 8, D], BF16, name="x_sb")
+            nc.sync.dma_start(out=x_sb[:], in_=query[b].rearrange("(p t) k -> p t k", t=8))
+            c_sb = xin.tile([P, 4, D], BF16, name="c_sb")
+            nc.sync.dma_start(out=c_sb[:], in_=context[b].rearrange("(t p) k -> p t k", p=P))
+            x_tiles[b] = x_sb
+            c_tiles[b] = c_sb
+
         load(0)
         load(1)
 
@@ -79,9 +71,12 @@ def tile_attention_pa_t_kernel(tc, query, context, query_bit, context_bit, W_in,
             out=pa[:], in0=qb_bf[:].rearrange("p b t -> p (b t)"), scalar1=10000.0, scalar2=None, op0=ALU.mult
         )
         dead = const.tile([P, B * K], BF16, name="dead")
+        nc.vector.tensor_scalar(
+            out=dead[:], in0=cb_all[:], scalar1=-1.0, scalar2=1.0, op0=ALU.mult, op1=ALU.add
+        )
 
-        def transposes(src_f32, grouped_f32):
-            for h in range(2):
+        def transpose_group(src_f32, n_tiles, grouped_f32):
+            for h in range(n_tiles // 2):
                 tp = ps_t.tile([P, 4, P], F32, name="tp")
                 for a in range(2):
                     for u in range(2):
@@ -93,39 +88,41 @@ def tile_attention_pa_t_kernel(tc, query, context, query_bit, context_bit, W_in,
                     in_=tp[:].rearrange("p (a u) m -> p a m u", a=2),
                 )
 
-        def quantise(grouped, codes, scales):
-            nc.vector.quantize_mx(
-                out=codes[:].bitcast(FP8X4), scales=scales[:], in_=grouped[:].rearrange("p t m v -> p (t m v)")
-            )
-
         Wg = const.tile([P, 4, P, 4], BF16, name="Wg", align_bytes=64)
         Wc = const.tile([P, 4 * P], U32, name="Wc", align_bytes=64)
         Ws = const.tile([P, 4 * P], U8, name="Ws", align_bytes=64)
-        transposes(W_sb[:].bitcast(F32), Wg[:].bitcast(F32))
-        quantise(Wg, Wc, Ws)
+        transpose_group(W_sb[:].bitcast(F32), 4, Wg[:].bitcast(F32))
+        nc.vector.quantize_mx(
+            out=Wc[:].bitcast(FP8X4), scales=Ws[:], in_=Wg[:].rearrange("p t m v -> p (t m v)")
+        )
 
-        def x_transpose(n):
+        ctx_q = {}
+        x_q = {}
+        q_q = {}
+
+        def stage_ctx(b):
+            cg = work.tile([P, 4, P, 4], BF16, name="cg", align_bytes=64)
+            cc = work.tile([P, K], U32, name="cc", align_bytes=64)
+            cs = work.tile([P, K], U8, name="cs", align_bytes=64)
+            transpose_group(c_tiles[b][:].bitcast(F32), 4, cg[:].bitcast(F32))
+            nc.vector.quantize_mx(
+                out=cc[:].bitcast(FP8X4), scales=cs[:], in_=cg[:].rearrange("p t m v -> p (t m v)")
+            )
+            ctx_q[b] = (cc, cs)
+
+        def stage_x(n):
+            b, h = n // 2, n % 2
             xg = work.tile([P, 4, P, 4], BF16, name="xg", align_bytes=64)
-            transposes(x_in[n][:].bitcast(F32), xg[:].bitcast(F32))
-            x_grp[n] = xg
-            if n % 2 == 0:
-                cg = work.tile([P, 4, P, 4], BF16, name="cg", align_bytes=64)
-                transposes(c_in[n // 2][:].bitcast(F32), cg[:].bitcast(F32))
-                c_grp[n // 2] = cg
-
-        def x_quantise(n):
             xc = work.tile([P, 512], U32, name="xc", align_bytes=64)
             xs = work.tile([P, 512], U8, name="xs", align_bytes=64)
-            quantise(x_grp[n], xc, xs)
-            x_mx[n] = (xc, xs)
-            if n % 2 == 0:
-                cc = keep.tile([P, K], U32, name="cc", align_bytes=64)
-                cs = keep.tile([P, K], U8, name="cs", align_bytes=64)
-                quantise(c_grp[n // 2], cc, cs)
-                c_mx[n // 2] = (cc, cs)
+            transpose_group(x_tiles[b][:, 4 * h : 4 * h + 4, :].bitcast(F32), 4, xg[:].bitcast(F32))
+            nc.vector.quantize_mx(
+                out=xc[:].bitcast(FP8X4), scales=xs[:], in_=xg[:].rearrange("p t m v -> p (t m v)")
+            )
+            x_q[n] = (xc, xs)
 
-        def q_matmuls(n):
-            xc, xs = x_mx[n]
+        def stage_q(n):
+            xc, xs = x_q[n]
             q_bf = work.tile([P, 4, 512], BF16, name="q_bf")
             for t in range(4):
                 qp = ps_q.tile([P, 512], F32, name="qp")
@@ -141,28 +138,30 @@ def tile_attention_pa_t_kernel(tc, query, context, query_bit, context_bit, W_in,
                 nc.scalar.activation(
                     out=q_bf[:, t, :], in_=qp[:], func=ACT.Identity, bias=b_f[:, t : t + 1], scale=1.0
                 )
-            q_rows[n] = q_bf
-
-        def q_regroup(n):
             qg = work.tile([P, 512, 4], BF16, name="qg", align_bytes=64)
-            nc.vector.tensor_copy(
-                out=qg[:].rearrange("p (c i) t -> p c t i", i=4),
-                in_=q_rows[n][:].rearrange("p t (c i) -> p c t i", i=4),
+            qc = work.tile([P, 512], U32, name="qc", align_bytes=64)
+            qs = work.tile([P, 512], U8, name="qs", align_bytes=64)
+            nc.gpsimd.tensor_scalar(
+                out=qg[:],
+                in0=q_bf[:].rearrange("p t c -> p c t"),
+                scalar1=1.0,
+                scalar2=0.0,
+                op0=ALU.mult,
+                op1=ALU.add,
             )
-            q_grp[n] = qg
-
-        def q_quantise(n):
-            qc = keep.tile([P, 512], U32, name="qc", align_bytes=64)
-            qs = keep.tile([P, 512], U8, name="qs", align_bytes=64)
             nc.vector.quantize_mx(
-                out=qc[:].bitcast(FP8X4), scales=qs[:], in_=q_grp[n][:].rearrange("p c t -> p (c t)")
+                out=qc[:].bitcast(FP8X4), scales=qs[:], in_=qg[:].rearrange("p c t -> p (c t)")
             )
-            q_mx[n] = (qc, qs)
+            q_q[n] = (qc, qs)
 
-        def s_matmuls(n):
-            qc, qs = q_mx[n]
-            cc, cs = c_mx[n // 2]
-            s_ps[n] = []
+        def stage_s(n):
+            b, h = n // 2, n % 2
+            qc, qs = q_q[n]
+            cc, cs = ctx_q[b]
+            z = soft.tile([P, 4, K], F32, name="z")
+            nm = soft.tile([P, 4], F32, name="nm")
+            ssum = soft.tile([P, 4], F32, name="ssum")
+            r = soft.tile([P, 4], F32, name="r")
             for k in range(4):
                 sp = ps_s.tile([P, K], F32, name="sp")
                 nc.tensor.matmul_mx(
@@ -174,92 +173,48 @@ def tile_attention_pa_t_kernel(tc, query, context, query_bit, context_bit, W_in,
                     start=True,
                     stop=True,
                 )
-                s_ps[n].append(sp)
-
-        def normalise(n):
-            b, h = n // 2, n % 2
-            z = z_of[n]
-            rows = out[b].rearrange("(p t) j -> p t j", t=8)
-            r = soft.tile([P, 4], F32, name="r")
-            if n == UNITS - 1:
-                for k in range(4):
-                    nc.vector.reciprocal(out=r[:, k : k + 1], in_=sum_of[n][:, k : k + 1])
-                    nc.vector.tensor_scalar(
-                        out=z[:, k, :], in0=z[:, k, :], scalar1=r[:, k : k + 1], scalar2=None, op0=ALU.mult
-                    )
-                    nc.sync.dma_start(out=rows[:, 4 * h + k, :], in_=z[:, k, :])
-            else:
-                nc.vector.reciprocal(out=r[:], in_=sum_of[n][:])
-                for k in range(4):
-                    nc.gpsimd.tensor_scalar(
-                        out=z[:, k, :],
-                        in0=z[:, k, :],
-                        scalar1=r[:, k : k + 1],
-                        scalar2=0.0,
-                        op0=ALU.mult,
-                        op1=ALU.add,
-                    )
-                nc.sync.dma_start(out=rows[:, 4 * h : 4 * h + 4, :], in_=z[:])
-
-        def s_mask_min(n):
-            b = n // 2
-            z = soft.tile([P, 4, K], F32, name="z")
-            nm = soft.tile([P, 4], F32, name="nm")
-            z_of[n] = z
-            nm_of[n] = nm
-            for k in range(4):
-                col = 4 * n + k
+                col = 8 * b + 4 * h + k
                 nc.vector.scalar_tensor_tensor(
                     out=z[:, k, :],
                     in0=dead[:, K * b : K * (b + 1)],
                     scalar=pa[:, col : col + 1],
-                    in1=s_ps[n][k][:],
+                    in1=sp[:],
                     op0=ALU.mult,
                     op1=ALU.subtract,
                 )
-                if k == 0 and unit(n - 1):
-                    normalise(n - 1)
-                if n == UNITS - 1:
-                    nc.vector.tensor_reduce(out=nm[:, k : k + 1], in_=z[:, k, :], axis=AX.X, op=ALU.min)
-            if n != UNITS - 1:
-                nc.vector.tensor_reduce(out=nm[:], in_=z[:], axis=AX.X, op=ALU.min)
-
-        def s_exp(n):
-            z = z_of[n]
-            ssum = soft.tile([P, 4], F32, name="ssum")
-            sum_of[n] = ssum
+            nc.vector.tensor_reduce(out=nm[:], in_=z[:], axis=AX.X, op=ALU.min)
             for k in range(4):
                 nc.scalar.activation(
                     out=z[:, k, :],
                     in_=z[:, k, :],
                     func=ACT.Exp,
-                    bias=nm_of[n][:, k : k + 1],
+                    bias=nm[:, k : k + 1],
                     scale=-1.0,
                     accum_out=ssum[:, k : k + 1],
                 )
-
-        for n in range(-3, UNITS + 1):
-            if unit(n + 5):
-                load(n + 5)
-            if n == 0:
-                nc.vector.tensor_scalar(
-                    out=dead[:], in0=cb_all[:], scalar1=-1.0, scalar2=1.0, op0=ALU.mult, op1=ALU.add
+            nc.vector.reciprocal(out=r[:], in_=ssum[:])
+            for k in range(4):
+                nc.gpsimd.tensor_scalar(
+                    out=z[:, k, :],
+                    in0=z[:, k, :],
+                    scalar1=r[:, k : k + 1],
+                    scalar2=0.0,
+                    op0=ALU.mult,
+                    op1=ALU.add,
                 )
-            if unit(n):
-                s_mask_min(n)
-            if n == UNITS:
-                normalise(n - 1)
-            if unit(n + 2):
-                q_matmuls(n + 2)
-            if unit(n + 3):
-                x_transpose(n + 3)
-            if unit(n):
-                s_exp(n)
-            if unit(n + 1):
-                s_matmuls(n + 1)
-            if unit(n + 2):
-                q_regroup(n + 2)
-            if unit(n + 3):
-                x_quantise(n + 3)
-            if unit(n + 2):
-                q_quantise(n + 2)
+            nc.sync.dma_start(
+                out=out[b].rearrange("(p t) j -> p t j", t=8)[:, 4 * h : 4 * h + 4, :], in_=z[:]
+            )
+
+        for n in range(UNITS + 2):
+            if n < UNITS:
+                b, h = n // 2, n % 2
+                if h == 0:
+                    if b + 2 < B:
+                        load(b + 2)
+                    stage_ctx(b)
+                stage_x(n)
+            if 1 <= n <= UNITS:
+                stage_q(n - 1)
+            if n >= 2:
+                stage_s(n - 2)

@@ -141,13 +141,9 @@ def tile_attention_pa_t_kernel(tc, query, context, query_bit, context_bit, W_in,
             qg = work.tile([P, 512, 4], BF16, name="qg", align_bytes=64)
             qc = work.tile([P, 512], U32, name="qc", align_bytes=64)
             qs = work.tile([P, 512], U8, name="qs", align_bytes=64)
-            nc.gpsimd.tensor_scalar(
-                out=qg[:],
-                in0=q_bf[:].rearrange("p t c -> p c t"),
-                scalar1=1.0,
-                scalar2=0.0,
-                op0=ALU.mult,
-                op1=ALU.add,
+            nc.vector.tensor_copy(
+                out=qg[:].rearrange("p (c i) t -> p c t i", i=4),
+                in_=q_bf[:].rearrange("p t (c i) -> p c t i", i=4),
             )
             nc.vector.quantize_mx(
                 out=qc[:].bitcast(FP8X4), scales=qs[:], in_=qg[:].rearrange("p c t -> p (c t)")
@@ -194,14 +190,14 @@ def tile_attention_pa_t_kernel(tc, query, context, query_bit, context_bit, W_in,
                 )
             nc.vector.reciprocal(out=r[:], in_=ssum[:])
             for k in range(4):
-                nc.gpsimd.tensor_scalar(
-                    out=z[:, k, :],
-                    in0=z[:, k, :],
-                    scalar1=r[:, k : k + 1],
-                    scalar2=0.0,
-                    op0=ALU.mult,
-                    op1=ALU.add,
-                )
+                if k % 2 == 0:
+                    nc.vector.tensor_scalar(
+                        out=z[:, k, :], in0=z[:, k, :], scalar1=r[:, k : k + 1], scalar2=None, op0=ALU.mult
+                    )
+                else:
+                    nc.scalar.activation(
+                        out=z[:, k, :], in_=z[:, k, :], func=ACT.Copy, scale=r[:, k : k + 1]
+                    )
             nc.sync.dma_start(
                 out=out[b].rearrange("(p t) j -> p t j", t=8)[:, 4 * h : 4 * h + 4, :], in_=z[:]
             )

@@ -1,8 +1,6 @@
 from contextlib import ExitStack
 
-import concourse.bass as bass
 import concourse.mybir as mybir
-import concourse.tile as tile
 from concourse.masks import make_identity
 
 F32 = mybir.dt.float32
@@ -23,30 +21,40 @@ UNITS = 2 * B
 def tile_attention_pa_t_kernel(tc, query, context, query_bit, context_bit, W_in, b_in, out):
     nc = tc.nc
     with ExitStack() as ctx:
+        ctx.enter_context(tc.manual_schedule())
         const = ctx.enter_context(tc.tile_pool(name="const", bufs=1))
-        xin = ctx.enter_context(tc.tile_pool(name="xin", bufs=3))
+        xin = ctx.enter_context(tc.tile_pool(name="xin", bufs=4))
+        cin = ctx.enter_context(tc.tile_pool(name="cin", bufs=2))
         work = ctx.enter_context(tc.tile_pool(name="work", bufs=2))
-        soft = ctx.enter_context(tc.tile_pool(name="soft", bufs=4))
+        keep = ctx.enter_context(tc.tile_pool(name="keep", bufs=3))
+        soft = ctx.enter_context(tc.tile_pool(name="soft", bufs=5))
         ps_t = ctx.enter_context(tc.psum_pool(name="ps_t", bufs=2))
-        ps_q = ctx.enter_context(tc.psum_pool(name="ps_q", bufs=3))
-        ps_s = ctx.enter_context(tc.psum_pool(name="ps_s", bufs=3))
+        ps_q = ctx.enter_context(tc.psum_pool(name="ps_q", bufs=2))
+        ps_s = ctx.enter_context(tc.psum_pool(name="ps_s", bufs=4))
+
+        x_in, c_in, x_grp, c_grp, x_mx, c_mx = {}, {}, {}, {}, {}, {}
+        q_rows, q_grp, q_mx, s_ps, z_of, nm_of, sum_of = {}, {}, {}, {}, {}, {}, {}
+
+        def unit(n):
+            return 0 <= n < UNITS
+
+        def load(n):
+            b, h = n // 2, n % 2
+            x_sb = xin.tile([P, 4, D], BF16, name="x_sb")
+            nc.sync.dma_start(
+                out=x_sb[:], in_=query[b].rearrange("(p t) k -> p t k", t=8)[:, 4 * h : 4 * h + 4, :]
+            )
+            x_in[n] = x_sb
+            if h == 0:
+                c_sb = cin.tile([P, 4, D], BF16, name="c_sb")
+                nc.sync.dma_start(out=c_sb[:], in_=context[b].rearrange("(t p) k -> p t k", p=P))
+                c_in[b] = c_sb
 
         W_sb = const.tile([P, 4, D], BF16, name="W_sb")
         nc.sync.dma_start(
             out=W_sb[:].rearrange("m (u e) k -> m u (e k)", u=2),
             in_=W_in.rearrange("(u m e) k -> m u (e k)", u=2, e=2),
         )
-        x_tiles = {}
-        c_tiles = {}
-
-        def load(b):
-            x_sb = xin.tile([P, 8, D], BF16, name="x_sb")
-            nc.sync.dma_start(out=x_sb[:], in_=query[b].rearrange("(p t) k -> p t k", t=8))
-            c_sb = xin.tile([P, 4, D], BF16, name="c_sb")
-            nc.sync.dma_start(out=c_sb[:], in_=context[b].rearrange("(t p) k -> p t k", p=P))
-            x_tiles[b] = x_sb
-            c_tiles[b] = c_sb
-
         load(0)
         load(1)
 
@@ -71,12 +79,12 @@ def tile_attention_pa_t_kernel(tc, query, context, query_bit, context_bit, W_in,
             out=pa[:], in0=qb_bf[:].rearrange("p b t -> p (b t)"), scalar1=10000.0, scalar2=None, op0=ALU.mult
         )
         dead = const.tile([P, B * K], BF16, name="dead")
-        nc.vector.tensor_scalar(
+        nc.gpsimd.tensor_scalar(
             out=dead[:], in0=cb_all[:], scalar1=-1.0, scalar2=1.0, op0=ALU.mult, op1=ALU.add
         )
 
-        def transpose_group(src_f32, n_tiles, grouped_f32):
-            for h in range(n_tiles // 2):
+        def transposes(src_f32, grouped_f32):
+            for h in range(2):
                 tp = ps_t.tile([P, 4, P], F32, name="tp")
                 for a in range(2):
                     for u in range(2):
@@ -88,41 +96,39 @@ def tile_attention_pa_t_kernel(tc, query, context, query_bit, context_bit, W_in,
                     in_=tp[:].rearrange("p (a u) m -> p a m u", a=2),
                 )
 
+        def quantise(grouped, codes, scales):
+            nc.vector.quantize_mx(
+                out=codes[:].bitcast(FP8X4), scales=scales[:], in_=grouped[:].rearrange("p t m v -> p (t m v)")
+            )
+
         Wg = const.tile([P, 4, P, 4], BF16, name="Wg", align_bytes=64)
         Wc = const.tile([P, 4 * P], U32, name="Wc", align_bytes=64)
         Ws = const.tile([P, 4 * P], U8, name="Ws", align_bytes=64)
-        transpose_group(W_sb[:].bitcast(F32), 4, Wg[:].bitcast(F32))
-        nc.vector.quantize_mx(
-            out=Wc[:].bitcast(FP8X4), scales=Ws[:], in_=Wg[:].rearrange("p t m v -> p (t m v)")
-        )
+        transposes(W_sb[:].bitcast(F32), Wg[:].bitcast(F32))
+        quantise(Wg, Wc, Ws)
 
-        ctx_q = {}
-        x_q = {}
-        q_q = {}
-
-        def stage_ctx(b):
-            cg = work.tile([P, 4, P, 4], BF16, name="cg", align_bytes=64)
-            cc = work.tile([P, K], U32, name="cc", align_bytes=64)
-            cs = work.tile([P, K], U8, name="cs", align_bytes=64)
-            transpose_group(c_tiles[b][:].bitcast(F32), 4, cg[:].bitcast(F32))
-            nc.vector.quantize_mx(
-                out=cc[:].bitcast(FP8X4), scales=cs[:], in_=cg[:].rearrange("p t m v -> p (t m v)")
-            )
-            ctx_q[b] = (cc, cs)
-
-        def stage_x(n):
-            b, h = n // 2, n % 2
+        def x_transpose(n):
             xg = work.tile([P, 4, P, 4], BF16, name="xg", align_bytes=64)
+            transposes(x_in[n][:].bitcast(F32), xg[:].bitcast(F32))
+            x_grp[n] = xg
+            if n % 2 == 0:
+                cg = work.tile([P, 4, P, 4], BF16, name="cg", align_bytes=64)
+                transposes(c_in[n // 2][:].bitcast(F32), cg[:].bitcast(F32))
+                c_grp[n // 2] = cg
+
+        def x_quantise(n):
             xc = work.tile([P, 512], U32, name="xc", align_bytes=64)
             xs = work.tile([P, 512], U8, name="xs", align_bytes=64)
-            transpose_group(x_tiles[b][:, 4 * h : 4 * h + 4, :].bitcast(F32), 4, xg[:].bitcast(F32))
-            nc.vector.quantize_mx(
-                out=xc[:].bitcast(FP8X4), scales=xs[:], in_=xg[:].rearrange("p t m v -> p (t m v)")
-            )
-            x_q[n] = (xc, xs)
+            quantise(x_grp[n], xc, xs)
+            x_mx[n] = (xc, xs)
+            if n % 2 == 0:
+                cc = keep.tile([P, K], U32, name="cc", align_bytes=64)
+                cs = keep.tile([P, K], U8, name="cs", align_bytes=64)
+                quantise(c_grp[n // 2], cc, cs)
+                c_mx[n // 2] = (cc, cs)
 
-        def stage_q(n):
-            xc, xs = x_q[n]
+        def q_matmuls(n):
+            xc, xs = x_mx[n]
             q_bf = work.tile([P, 4, 512], BF16, name="q_bf")
             for t in range(4):
                 qp = ps_q.tile([P, 512], F32, name="qp")
@@ -138,26 +144,28 @@ def tile_attention_pa_t_kernel(tc, query, context, query_bit, context_bit, W_in,
                 nc.scalar.activation(
                     out=q_bf[:, t, :], in_=qp[:], func=ACT.Identity, bias=b_f[:, t : t + 1], scale=1.0
                 )
+            q_rows[n] = q_bf
+
+        def q_regroup(n):
             qg = work.tile([P, 512, 4], BF16, name="qg", align_bytes=64)
-            qc = work.tile([P, 512], U32, name="qc", align_bytes=64)
-            qs = work.tile([P, 512], U8, name="qs", align_bytes=64)
             nc.vector.tensor_copy(
                 out=qg[:].rearrange("p (c i) t -> p c t i", i=4),
-                in_=q_bf[:].rearrange("p t (c i) -> p c t i", i=4),
+                in_=q_rows[n][:].rearrange("p t (c i) -> p c t i", i=4),
             )
-            nc.vector.quantize_mx(
-                out=qc[:].bitcast(FP8X4), scales=qs[:], in_=qg[:].rearrange("p c t -> p (c t)")
-            )
-            q_q[n] = (qc, qs)
+            q_grp[n] = qg
 
-        def stage_s(n):
-            b, h = n // 2, n % 2
-            qc, qs = q_q[n]
-            cc, cs = ctx_q[b]
-            z = soft.tile([P, 4, K], F32, name="z")
-            nm = soft.tile([P, 4], F32, name="nm")
-            ssum = soft.tile([P, 4], F32, name="ssum")
-            r = soft.tile([P, 4], F32, name="r")
+        def q_quantise(n):
+            qc = keep.tile([P, 512], U32, name="qc", align_bytes=64)
+            qs = keep.tile([P, 512], U8, name="qs", align_bytes=64)
+            nc.vector.quantize_mx(
+                out=qc[:].bitcast(FP8X4), scales=qs[:], in_=q_grp[n][:].rearrange("p c t -> p (c t)")
+            )
+            q_mx[n] = (qc, qs)
+
+        def s_matmuls(n):
+            qc, qs = q_mx[n]
+            cc, cs = c_mx[n // 2]
+            s_ps[n] = []
             for k in range(4):
                 sp = ps_s.tile([P, K], F32, name="sp")
                 nc.tensor.matmul_mx(
@@ -169,48 +177,90 @@ def tile_attention_pa_t_kernel(tc, query, context, query_bit, context_bit, W_in,
                     start=True,
                     stop=True,
                 )
-                col = 8 * b + 4 * h + k
+                s_ps[n].append(sp)
+
+        def normalise(n):
+            b, h = n // 2, n % 2
+            z = z_of[n]
+            rows = out[b].rearrange("(p t) j -> p t j", t=8)
+            r = soft.tile([P, 4], F32, name="r")
+            if n == UNITS - 1:
+                for k in range(4):
+                    nc.vector.reciprocal(out=r[:, k : k + 1], in_=sum_of[n][:, k : k + 1])
+                    nc.vector.tensor_scalar(
+                        out=z[:, k, :], in0=z[:, k, :], scalar1=r[:, k : k + 1], scalar2=None, op0=ALU.mult
+                    )
+                    nc.sync.dma_start(out=rows[:, 4 * h + k, :], in_=z[:, k, :])
+            else:
+                nc.vector.reciprocal(out=r[:], in_=sum_of[n][:])
+                for k in range(4):
+                    nc.gpsimd.tensor_scalar(
+                        out=z[:, k, :],
+                        in0=z[:, k, :],
+                        scalar1=r[:, k : k + 1],
+                        scalar2=0.0,
+                        op0=ALU.mult,
+                        op1=ALU.add,
+                    )
+                nc.sync.dma_start(out=rows[:, 4 * h : 4 * h + 4, :], in_=z[:])
+
+        def s_mask_min(n):
+            b = n // 2
+            z = soft.tile([P, 4, K], F32, name="z")
+            nm = soft.tile([P, 4], F32, name="nm")
+            z_of[n] = z
+            nm_of[n] = nm
+            for k in range(4):
+                col = 4 * n + k
                 nc.vector.scalar_tensor_tensor(
                     out=z[:, k, :],
                     in0=dead[:, K * b : K * (b + 1)],
                     scalar=pa[:, col : col + 1],
-                    in1=sp[:],
+                    in1=s_ps[n][k][:],
                     op0=ALU.mult,
                     op1=ALU.subtract,
                 )
-            nc.vector.tensor_reduce(out=nm[:], in_=z[:], axis=AX.X, op=ALU.min)
+                if k == 0 and unit(n - 2):
+                    normalise(n - 2)
+                if k == 2 and n == UNITS - 1:
+                    normalise(n - 1)
+                if n == UNITS - 1:
+                    nc.vector.tensor_reduce(out=nm[:, k : k + 1], in_=z[:, k, :], axis=AX.X, op=ALU.min)
+            if n != UNITS - 1:
+                nc.vector.tensor_reduce(out=nm[:], in_=z[:], axis=AX.X, op=ALU.min)
+
+        def s_exp(n):
+            z = z_of[n]
+            ssum = soft.tile([P, 4], F32, name="ssum")
+            sum_of[n] = ssum
             for k in range(4):
                 nc.scalar.activation(
                     out=z[:, k, :],
                     in_=z[:, k, :],
                     func=ACT.Exp,
-                    bias=nm[:, k : k + 1],
+                    bias=nm_of[n][:, k : k + 1],
                     scale=-1.0,
                     accum_out=ssum[:, k : k + 1],
                 )
-            nc.vector.reciprocal(out=r[:], in_=ssum[:])
-            for k in range(4):
-                if k % 2 == 0:
-                    nc.vector.tensor_scalar(
-                        out=z[:, k, :], in0=z[:, k, :], scalar1=r[:, k : k + 1], scalar2=None, op0=ALU.mult
-                    )
-                else:
-                    nc.scalar.activation(
-                        out=z[:, k, :], in_=z[:, k, :], func=ACT.Copy, scale=r[:, k : k + 1]
-                    )
-            nc.sync.dma_start(
-                out=out[b].rearrange("(p t) j -> p t j", t=8)[:, 4 * h : 4 * h + 4, :], in_=z[:]
-            )
 
-        for n in range(UNITS + 2):
-            if n < UNITS:
-                b, h = n // 2, n % 2
-                if h == 0:
-                    if b + 2 < B:
-                        load(b + 2)
-                    stage_ctx(b)
-                stage_x(n)
-            if 1 <= n <= UNITS:
-                stage_q(n - 1)
-            if n >= 2:
-                stage_s(n - 2)
+        for n in range(-3, UNITS + 1):
+            if unit(n + 5):
+                load(n + 5)
+            if unit(n):
+                s_mask_min(n)
+            if n == UNITS:
+                normalise(n - 1)
+            if unit(n + 2):
+                q_matmuls(n + 2)
+            if unit(n + 3):
+                x_transpose(n + 3)
+            if unit(n):
+                s_exp(n)
+            if unit(n + 1):
+                s_matmuls(n + 1)
+            if unit(n + 2):
+                q_regroup(n + 2)
+            if unit(n + 3):
+                x_quantise(n + 3)
+            if unit(n + 2):
+                q_quantise(n + 2)

@@ -1,6 +1,8 @@
 from contextlib import ExitStack
 
+import concourse.bass as bass
 import concourse.mybir as mybir
+import concourse.tile as tile
 from concourse.masks import make_identity
 
 F32 = mybir.dt.float32
@@ -21,40 +23,30 @@ UNITS = 2 * B
 def tile_attention_pa_t_kernel(tc, query, context, query_bit, context_bit, W_in, b_in, out):
     nc = tc.nc
     with ExitStack() as ctx:
-        ctx.enter_context(tc.manual_schedule())
         const = ctx.enter_context(tc.tile_pool(name="const", bufs=1))
-        xin = ctx.enter_context(tc.tile_pool(name="xin", bufs=4))
-        cin = ctx.enter_context(tc.tile_pool(name="cin", bufs=2))
+        xin = ctx.enter_context(tc.tile_pool(name="xin", bufs=3))
         work = ctx.enter_context(tc.tile_pool(name="work", bufs=2))
-        keep = ctx.enter_context(tc.tile_pool(name="keep", bufs=3))
-        soft = ctx.enter_context(tc.tile_pool(name="soft", bufs=5))
+        soft = ctx.enter_context(tc.tile_pool(name="soft", bufs=4))
         ps_t = ctx.enter_context(tc.psum_pool(name="ps_t", bufs=2))
-        ps_q = ctx.enter_context(tc.psum_pool(name="ps_q", bufs=2))
-        ps_s = ctx.enter_context(tc.psum_pool(name="ps_s", bufs=4))
-
-        x_in, c_in, x_grp, c_grp, x_mx, c_mx = {}, {}, {}, {}, {}, {}
-        q_rows, q_grp, q_mx, s_ps, z_of, nm_of, sum_of = {}, {}, {}, {}, {}, {}, {}
-
-        def unit(n):
-            return 0 <= n < UNITS
-
-        def load(n):
-            b, h = n // 2, n % 2
-            x_sb = xin.tile([P, 4, D], BF16, name="x_sb")
-            nc.sync.dma_start(
-                out=x_sb[:], in_=query[b].rearrange("(p t) k -> p t k", t=8)[:, 4 * h : 4 * h + 4, :]
-            )
-            x_in[n] = x_sb
-            if h == 0:
-                c_sb = cin.tile([P, 4, D], BF16, name="c_sb")
-                nc.sync.dma_start(out=c_sb[:], in_=context[b].rearrange("(t p) k -> p t k", p=P))
-                c_in[b] = c_sb
+        ps_q = ctx.enter_context(tc.psum_pool(name="ps_q", bufs=3))
+        ps_s = ctx.enter_context(tc.psum_pool(name="ps_s", bufs=3))
 
         W_sb = const.tile([P, 4, D], BF16, name="W_sb")
         nc.sync.dma_start(
             out=W_sb[:].rearrange("m (u e) k -> m u (e k)", u=2),
             in_=W_in.rearrange("(u m e) k -> m u (e k)", u=2, e=2),
         )
+        x_tiles = {}
+        c_tiles = {}
+
+        def load(b):
+            x_sb = xin.tile([P, 8, D], BF16, name="x_sb")
+            nc.sync.dma_start(out=x_sb[:], in_=query[b].rearrange("(p t) k -> p t k", t=8))
+            c_sb = xin.tile([P, 4, D], BF16, name="c_sb")
+            nc.sync.dma_start(out=c_sb[:], in_=context[b].rearrange("(t p) k -> p t k", p=P))
+            x_tiles[b] = x_sb
+            c_tiles[b] = c_sb
+
         load(0)
         load(1)
 
@@ -79,12 +71,12 @@ def tile_attention_pa_t_kernel(tc, query, context, query_bit, context_bit, W_in,
             out=pa[:], in0=qb_bf[:].rearrange("p b t -> p (b t)"), scalar1=10000.0, scalar2=None, op0=ALU.mult
         )
         dead = const.tile([P, B * K], BF16, name="dead")
-        nc.gpsimd.tensor_scalar(
+        nc.vector.tensor_scalar(
             out=dead[:], in0=cb_all[:], scalar1=-1.0, scalar2=1.0, op0=ALU.mult, op1=ALU.add
         )
 
-        def transposes(src_f32, grouped_f32):
-            for h in range(2):
+        def transpose_group(src_f32, n_tiles, grouped_f32):
+            for h in range(n_tiles // 2):
                 tp = ps_t.tile([P, 4, P], F32, name="tp")
                 for a in range(2):
                     for u in range(2):
@@ -96,39 +88,41 @@ def tile_attention_pa_t_kernel(tc, query, context, query_bit, context_bit, W_in,
                     in_=tp[:].rearrange("p (a u) m -> p a m u", a=2),
                 )
 
-        def quantise(grouped, codes, scales):
-            nc.vector.quantize_mx(
-                out=codes[:].bitcast(FP8X4), scales=scales[:], in_=grouped[:].rearrange("p t m v -> p (t m v)")
-            )
-
         Wg = const.tile([P, 4, P, 4], BF16, name="Wg", align_bytes=64)
         Wc = const.tile([P, 4 * P], U32, name="Wc", align_bytes=64)
         Ws = const.tile([P, 4 * P], U8, name="Ws", align_bytes=64)
-        transposes(W_sb[:].bitcast(F32), Wg[:].bitcast(F32))
-        quantise(Wg, Wc, Ws)
+        transpose_group(W_sb[:].bitcast(F32), 4, Wg[:].bitcast(F32))
+        nc.vector.quantize_mx(
+            out=Wc[:].bitcast(FP8X4), scales=Ws[:], in_=Wg[:].rearrange("p t m v -> p (t m v)")
+        )
 
-        def x_transpose(n):
+        ctx_q = {}
+        x_q = {}
+        q_q = {}
+
+        def stage_ctx(b):
+            cg = work.tile([P, 4, P, 4], BF16, name="cg", align_bytes=64)
+            cc = work.tile([P, K], U32, name="cc", align_bytes=64)
+            cs = work.tile([P, K], U8, name="cs", align_bytes=64)
+            transpose_group(c_tiles[b][:].bitcast(F32), 4, cg[:].bitcast(F32))
+            nc.vector.quantize_mx(
+                out=cc[:].bitcast(FP8X4), scales=cs[:], in_=cg[:].rearrange("p t m v -> p (t m v)")
+            )
+            ctx_q[b] = (cc, cs)
+
+        def stage_x(n):
+            b, h = n // 2, n % 2
             xg = work.tile([P, 4, P, 4], BF16, name="xg", align_bytes=64)
-            transposes(x_in[n][:].bitcast(F32), xg[:].bitcast(F32))
-            x_grp[n] = xg
-            if n % 2 == 0:
-                cg = work.tile([P, 4, P, 4], BF16, name="cg", align_bytes=64)
-                transposes(c_in[n // 2][:].bitcast(F32), cg[:].bitcast(F32))
-                c_grp[n // 2] = cg
-
-        def x_quantise(n):
             xc = work.tile([P, 512], U32, name="xc", align_bytes=64)
             xs = work.tile([P, 512], U8, name="xs", align_bytes=64)
-            quantise(x_grp[n], xc, xs)
-            x_mx[n] = (xc, xs)
-            if n % 2 == 0:
-                cc = keep.tile([P, K], U32, name="cc", align_bytes=64)
-                cs = keep.tile([P, K], U8, name="cs", align_bytes=64)
-                quantise(c_grp[n // 2], cc, cs)
-                c_mx[n // 2] = (cc, cs)
+            transpose_group(x_tiles[b][:, 4 * h : 4 * h + 4, :].bitcast(F32), 4, xg[:].bitcast(F32))
+            nc.vector.quantize_mx(
+                out=xc[:].bitcast(FP8X4), scales=xs[:], in_=xg[:].rearrange("p t m v -> p (t m v)")
+            )
+            x_q[n] = (xc, xs)
 
-        def q_matmuls(n):
-            xc, xs = x_mx[n]
+        def stage_q(n):
+            xc, xs = x_q[n]
             q_bf = work.tile([P, 4, 512], BF16, name="q_bf")
             for t in range(4):
                 qp = ps_q.tile([P, 512], F32, name="qp")
@@ -144,28 +138,30 @@ def tile_attention_pa_t_kernel(tc, query, context, query_bit, context_bit, W_in,
                 nc.scalar.activation(
                     out=q_bf[:, t, :], in_=qp[:], func=ACT.Identity, bias=b_f[:, t : t + 1], scale=1.0
                 )
-            q_rows[n] = q_bf
-
-        def q_regroup(n):
             qg = work.tile([P, 512, 4], BF16, name="qg", align_bytes=64)
+            qc = work.tile([P, 512], U32, name="qc", align_bytes=64)
+            qs = work.tile([P, 512], U8, name="qs", align_bytes=64)
+            nc.scalar.copy(
+                out=qg[:, 0:192, :].rearrange("p (c i) t -> p c t i", i=4),
+                in_=q_bf[:, :, 0:192].rearrange("p t (c i) -> p c t i", i=4),
+            )
             nc.vector.tensor_copy(
-                out=qg[:].rearrange("p (c i) t -> p c t i", i=4),
-                in_=q_rows[n][:].rearrange("p t (c i) -> p c t i", i=4),
+                out=qg[:, 192:512, :].rearrange("p (c i) t -> p c t i", i=4),
+                in_=q_bf[:, :, 192:512].rearrange("p t (c i) -> p c t i", i=4),
             )
-            q_grp[n] = qg
-
-        def q_quantise(n):
-            qc = keep.tile([P, 512], U32, name="qc", align_bytes=64)
-            qs = keep.tile([P, 512], U8, name="qs", align_bytes=64)
             nc.vector.quantize_mx(
-                out=qc[:].bitcast(FP8X4), scales=qs[:], in_=q_grp[n][:].rearrange("p c t -> p (c t)")
+                out=qc[:].bitcast(FP8X4), scales=qs[:], in_=qg[:].rearrange("p c t -> p (c t)")
             )
-            q_mx[n] = (qc, qs)
+            q_q[n] = (qc, qs)
 
-        def s_matmuls(n):
-            qc, qs = q_mx[n]
-            cc, cs = c_mx[n // 2]
-            s_ps[n] = []
+        def stage_s(n):
+            b, h = n // 2, n % 2
+            qc, qs = q_q[n]
+            cc, cs = ctx_q[b]
+            z = soft.tile([P, 4, K], F32, name="z")
+            nm = soft.tile([P, 4], F32, name="nm")
+            ssum = soft.tile([P, 4], F32, name="ssum")
+            r = soft.tile([P, 4], F32, name="r")
             for k in range(4):
                 sp = ps_s.tile([P, K], F32, name="sp")
                 nc.tensor.matmul_mx(
@@ -177,90 +173,48 @@ def tile_attention_pa_t_kernel(tc, query, context, query_bit, context_bit, W_in,
                     start=True,
                     stop=True,
                 )
-                s_ps[n].append(sp)
-
-        def normalise(n):
-            b, h = n // 2, n % 2
-            z = z_of[n]
-            rows = out[b].rearrange("(p t) j -> p t j", t=8)
-            r = soft.tile([P, 4], F32, name="r")
-            if n == UNITS - 1:
-                for k in range(4):
-                    nc.vector.reciprocal(out=r[:, k : k + 1], in_=sum_of[n][:, k : k + 1])
-                    nc.vector.tensor_scalar(
-                        out=z[:, k, :], in0=z[:, k, :], scalar1=r[:, k : k + 1], scalar2=None, op0=ALU.mult
-                    )
-                    nc.sync.dma_start(out=rows[:, 4 * h + k, :], in_=z[:, k, :])
-            else:
-                nc.vector.reciprocal(out=r[:], in_=sum_of[n][:])
-                for k in range(4):
-                    nc.gpsimd.tensor_scalar(
-                        out=z[:, k, :],
-                        in0=z[:, k, :],
-                        scalar1=r[:, k : k + 1],
-                        scalar2=0.0,
-                        op0=ALU.mult,
-                        op1=ALU.add,
-                    )
-                nc.sync.dma_start(out=rows[:, 4 * h : 4 * h + 4, :], in_=z[:])
-
-        def s_mask_min(n):
-            b = n // 2
-            z = soft.tile([P, 4, K], F32, name="z")
-            nm = soft.tile([P, 4], F32, name="nm")
-            z_of[n] = z
-            nm_of[n] = nm
-            for k in range(4):
-                col = 4 * n + k
+                col = 8 * b + 4 * h + k
                 nc.vector.scalar_tensor_tensor(
                     out=z[:, k, :],
                     in0=dead[:, K * b : K * (b + 1)],
                     scalar=pa[:, col : col + 1],
-                    in1=s_ps[n][k][:],
+                    in1=sp[:],
                     op0=ALU.mult,
                     op1=ALU.subtract,
                 )
-                if k == 0 and unit(n - 2):
-                    normalise(n - 2)
-                if k == 2 and n == UNITS - 1:
-                    normalise(n - 1)
-                if n == UNITS - 1:
-                    nc.vector.tensor_reduce(out=nm[:, k : k + 1], in_=z[:, k, :], axis=AX.X, op=ALU.min)
-            if n != UNITS - 1:
-                nc.vector.tensor_reduce(out=nm[:], in_=z[:], axis=AX.X, op=ALU.min)
-
-        def s_exp(n):
-            z = z_of[n]
-            ssum = soft.tile([P, 4], F32, name="ssum")
-            sum_of[n] = ssum
+            nc.vector.tensor_reduce(out=nm[:], in_=z[:], axis=AX.X, op=ALU.min)
             for k in range(4):
                 nc.scalar.activation(
                     out=z[:, k, :],
                     in_=z[:, k, :],
                     func=ACT.Exp,
-                    bias=nm_of[n][:, k : k + 1],
+                    bias=nm[:, k : k + 1],
                     scale=-1.0,
                     accum_out=ssum[:, k : k + 1],
                 )
+            nc.vector.reciprocal(out=r[:], in_=ssum[:])
+            for k in range(4):
+                nc.gpsimd.tensor_scalar(
+                    out=z[:, k, :],
+                    in0=z[:, k, :],
+                    scalar1=r[:, k : k + 1],
+                    scalar2=0.0,
+                    op0=ALU.mult,
+                    op1=ALU.add,
+                )
+            nc.sync.dma_start(
+                out=out[b].rearrange("(p t) j -> p t j", t=8)[:, 4 * h : 4 * h + 4, :], in_=z[:]
+            )
 
-        for n in range(-3, UNITS + 1):
-            if unit(n + 5):
-                load(n + 5)
-            if unit(n):
-                s_mask_min(n)
-            if n == UNITS:
-                normalise(n - 1)
-            if unit(n + 2):
-                q_matmuls(n + 2)
-            if unit(n + 3):
-                x_transpose(n + 3)
-            if unit(n):
-                s_exp(n)
-            if unit(n + 1):
-                s_matmuls(n + 1)
-            if unit(n + 2):
-                q_regroup(n + 2)
-            if unit(n + 3):
-                x_quantise(n + 3)
-            if unit(n + 2):
-                q_quantise(n + 2)
+        for n in range(UNITS + 2):
+            if n < UNITS:
+                b, h = n // 2, n % 2
+                if h == 0:
+                    if b + 2 < B:
+                        load(b + 2)
+                    stage_ctx(b)
+                stage_x(n)
+            if 1 <= n <= UNITS:
+                stage_q(n - 1)
+            if n >= 2:
+                stage_s(n - 2)

@@ -156,6 +156,7 @@ def tile_attention_pa_t_kernel(tc, query, context, query_bit, context_bit, W_in,
 
         def stage_s(n):
             b, h = n // 2, n % 2
+            last = n == UNITS - 1
             qc, qs = q_q[n]
             cc, cs = ctx_q[b]
             z = soft.tile([P, 4, K], F32, name="z")
@@ -182,7 +183,10 @@ def tile_attention_pa_t_kernel(tc, query, context, query_bit, context_bit, W_in,
                     op0=ALU.mult,
                     op1=ALU.subtract,
                 )
-            nc.vector.tensor_reduce(out=nm[:], in_=z[:], axis=AX.X, op=ALU.min)
+                if last:
+                    nc.vector.tensor_reduce(out=nm[:, k : k + 1], in_=z[:, k, :], axis=AX.X, op=ALU.min)
+            if not last:
+                nc.vector.tensor_reduce(out=nm[:], in_=z[:], axis=AX.X, op=ALU.min)
             for k in range(4):
                 nc.scalar.activation(
                     out=z[:, k, :],
@@ -192,19 +196,26 @@ def tile_attention_pa_t_kernel(tc, query, context, query_bit, context_bit, W_in,
                     scale=-1.0,
                     accum_out=ssum[:, k : k + 1],
                 )
-            nc.vector.reciprocal(out=r[:], in_=ssum[:])
-            for k in range(4):
-                nc.gpsimd.tensor_scalar(
-                    out=z[:, k, :],
-                    in0=z[:, k, :],
-                    scalar1=r[:, k : k + 1],
-                    scalar2=0.0,
-                    op0=ALU.mult,
-                    op1=ALU.add,
-                )
-            nc.sync.dma_start(
-                out=out[b].rearrange("(p t) j -> p t j", t=8)[:, 4 * h : 4 * h + 4, :], in_=z[:]
-            )
+            rows = out[b].rearrange("(p t) j -> p t j", t=8)
+            if last:
+                for k in range(4):
+                    nc.vector.reciprocal(out=r[:, k : k + 1], in_=ssum[:, k : k + 1])
+                    nc.vector.tensor_scalar(
+                        out=z[:, k, :], in0=z[:, k, :], scalar1=r[:, k : k + 1], scalar2=None, op0=ALU.mult
+                    )
+                    nc.sync.dma_start(out=rows[:, 4 * h + k, :], in_=z[:, k, :])
+            else:
+                nc.vector.reciprocal(out=r[:], in_=ssum[:])
+                for k in range(4):
+                    nc.gpsimd.tensor_scalar(
+                        out=z[:, k, :],
+                        in0=z[:, k, :],
+                        scalar1=r[:, k : k + 1],
+                        scalar2=0.0,
+                        op0=ALU.mult,
+                        op1=ALU.add,
+                    )
+                nc.sync.dma_start(out=rows[:, 4 * h : 4 * h + 4, :], in_=z[:])
 
         for n in range(UNITS + 2):
             if n < UNITS:

from contextlib import ExitStack

import concourse.bass as bass
import concourse.mybir as mybir
import concourse.tile as tile
from concourse.masks import make_identity

F32 = mybir.dt.float32
BF16 = mybir.dt.bfloat16
U32 = mybir.dt.uint32
U8 = mybir.dt.uint8
FP8X4 = mybir.dt.float8_e4m3fn_x4
ALU = mybir.AluOpType
ACT = mybir.ActivationFunctionType
AX = mybir.AxisListType

P = 128
B, Q, K, D = 8, 1024, 512, 512
FLOPS = 2 * (2 * B * Q * D * D)
UNITS = 2 * B


def tile_attention_pa_t_kernel(tc, query, context, query_bit, context_bit, W_in, b_in, out):
    nc = tc.nc
    with ExitStack() as ctx:
        const = ctx.enter_context(tc.tile_pool(name="const", bufs=1))
        xin = ctx.enter_context(tc.tile_pool(name="xin", bufs=3))
        work = ctx.enter_context(tc.tile_pool(name="work", bufs=2))
        soft = ctx.enter_context(tc.tile_pool(name="soft", bufs=4))
        ps_t = ctx.enter_context(tc.psum_pool(name="ps_t", bufs=2))
        ps_q = ctx.enter_context(tc.psum_pool(name="ps_q", bufs=3))
        ps_s = ctx.enter_context(tc.psum_pool(name="ps_s", bufs=3))

        W_sb = const.tile([P, 4, D], BF16, name="W_sb")
        nc.sync.dma_start(
            out=W_sb[:].rearrange("m (u e) k -> m u (e k)", u=2),
            in_=W_in.rearrange("(u m e) k -> m u (e k)", u=2, e=2),
        )
        x_tiles = {}
        c_tiles = {}

        def load(b):
            x_sb = xin.tile([P, 8, D], BF16, name="x_sb")
            nc.sync.dma_start(out=x_sb[:], in_=query[b].rearrange("(p t) k -> p t k", t=8))
            c_sb = xin.tile([P, 4, D], BF16, name="c_sb")
            nc.sync.dma_start(out=c_sb[:], in_=context[b].rearrange("(t p) k -> p t k", p=P))
            x_tiles[b] = x_sb
            c_tiles[b] = c_sb

        load(0)
        load(1)

        ident = const.tile([P, P], F32, name="ident")
        make_identity(nc, ident[:])

        b_bf = const.tile([P, 4], BF16, name="b_bf")
        qb_bf = const.tile([P, B, 8], BF16, name="qb_bf")
        with nc.allow_non_contiguous_dma(reason="two small vectors, loaded once"):
            nc.scalar.dma_start(
                out=b_bf[:].rearrange("m (u e) -> m u e", u=2),
                in_=b_in.rearrange("(u m e) -> m u e", u=2, e=2),
            )
            nc.scalar.dma_start(out=qb_bf[:], in_=query_bit.rearrange("b (p t) -> p b t", t=8))
        cb_all = const.tile([P, B * K], BF16, name="cb_all")
        nc.scalar.dma_start(out=cb_all[:], in_=context_bit.rearrange("b j -> (b j)").partition_broadcast(P))

        b_f = const.tile([P, 4], F32, name="b_f")
        nc.vector.tensor_copy(out=b_f[:], in_=b_bf[:])
        pa = const.tile([P, B * 8], F32, name="pa")
        nc.vector.tensor_scalar(
            out=pa[:], in0=qb_bf[:].rearrange("p b t -> p (b t)"), scalar1=10000.0, scalar2=None, op0=ALU.mult
        )
        dead = const.tile([P, B * K], BF16, name="dead")
        nc.vector.tensor_scalar(
            out=dead[:], in0=cb_all[:], scalar1=-1.0, scalar2=1.0, op0=ALU.mult, op1=ALU.add
        )

        def transpose_group(src_f32, n_tiles, grouped_f32):
            for h in range(n_tiles // 2):
                tp = ps_t.tile([P, 4, P], F32, name="tp")
                for a in range(2):
                    for u in range(2):
                        nc.tensor.transpose(
                            tp[:, 2 * a + u, :], src_f32[:, 2 * h + a, P * u : P * (u + 1)], ident[:]
                        )
                nc.scalar.copy(
                    out=grouped_f32[:, 2 * h : 2 * h + 2, :, :],
                    in_=tp[:].rearrange("p (a u) m -> p a m u", a=2),
                )

        Wg = const.tile([P, 4, P, 4], BF16, name="Wg", align_bytes=64)
        Wc = const.tile([P, 4 * P], U32, name="Wc", align_bytes=64)
        Ws = const.tile([P, 4 * P], U8, name="Ws", align_bytes=64)
        transpose_group(W_sb[:].bitcast(F32), 4, Wg[:].bitcast(F32))
        nc.vector.quantize_mx(
            out=Wc[:].bitcast(FP8X4), scales=Ws[:], in_=Wg[:].rearrange("p t m v -> p (t m v)")
        )

        ctx_q = {}
        x_q = {}
        q_q = {}

        def stage_ctx(b):
            cg = work.tile([P, 4, P, 4], BF16, name="cg", align_bytes=64)
            cc = work.tile([P, K], U32, name="cc", align_bytes=64)
            cs = work.tile([P, K], U8, name="cs", align_bytes=64)
            transpose_group(c_tiles[b][:].bitcast(F32), 4, cg[:].bitcast(F32))
            nc.vector.quantize_mx(
                out=cc[:].bitcast(FP8X4), scales=cs[:], in_=cg[:].rearrange("p t m v -> p (t m v)")
            )
            ctx_q[b] = (cc, cs)

        def stage_x(n):
            b, h = n // 2, n % 2
            xg = work.tile([P, 4, P, 4], BF16, name="xg", align_bytes=64)
            xc = work.tile([P, 512], U32, name="xc", align_bytes=64)
            xs = work.tile([P, 512], U8, name="xs", align_bytes=64)
            transpose_group(x_tiles[b][:, 4 * h : 4 * h + 4, :].bitcast(F32), 4, xg[:].bitcast(F32))
            nc.vector.quantize_mx(
                out=xc[:].bitcast(FP8X4), scales=xs[:], in_=xg[:].rearrange("p t m v -> p (t m v)")
            )
            x_q[n] = (xc, xs)

        def stage_q(n):
            xc, xs = x_q[n]
            q_bf = work.tile([P, 4, 512], BF16, name="q_bf")
            for t in range(4):
                qp = ps_q.tile([P, 512], F32, name="qp")
                nc.tensor.matmul_mx(
                    out=qp[:],
                    lhsT=Wc[:, P * t : P * (t + 1)].bitcast(FP8X4),
                    lhsT_scale=Ws[:, P * t : P * (t + 1)],
                    rhs=xc[:].bitcast(FP8X4),
                    rhs_scale=xs[:],
                    start=True,
                    stop=True,
                )
                nc.scalar.activation(
                    out=q_bf[:, t, :], in_=qp[:], func=ACT.Identity, bias=b_f[:, t : t + 1], scale=1.0
                )
            qg = work.tile([P, 512, 4], BF16, name="qg", align_bytes=64)
            qc = work.tile([P, 512], U32, name="qc", align_bytes=64)
            qs = work.tile([P, 512], U8, name="qs", align_bytes=64)
            nc.scalar.copy(
                out=qg[:, 0:192, :].rearrange("p (c i) t -> p c t i", i=4),
                in_=q_bf[:, :, 0:192].rearrange("p t (c i) -> p c t i", i=4),
            )
            nc.vector.tensor_copy(
                out=qg[:, 192:512, :].rearrange("p (c i) t -> p c t i", i=4),
                in_=q_bf[:, :, 192:512].rearrange("p t (c i) -> p c t i", i=4),
            )
            nc.vector.quantize_mx(
                out=qc[:].bitcast(FP8X4), scales=qs[:], in_=qg[:].rearrange("p c t -> p (c t)")
            )
            q_q[n] = (qc, qs)

        def stage_s(n):
            b, h = n // 2, n % 2
            last = n == UNITS - 1
            qc, qs = q_q[n]
            cc, cs = ctx_q[b]
            z = soft.tile([P, 4, K], F32, name="z")
            nm = soft.tile([P, 4], F32, name="nm")
            ssum = soft.tile([P, 4], F32, name="ssum")
            r = soft.tile([P, 4], F32, name="r")
            for k in range(4):
                sp = ps_s.tile([P, K], F32, name="sp")
                nc.tensor.matmul_mx(
                    out=sp[:],
                    lhsT=qc[:, P * k : P * (k + 1)].bitcast(FP8X4),
                    lhsT_scale=qs[:, P * k : P * (k + 1)],
                    rhs=cc[:].bitcast(FP8X4),
                    rhs_scale=cs[:],
                    start=True,
                    stop=True,
                )
                col = 8 * b + 4 * h + k
                nc.vector.scalar_tensor_tensor(
                    out=z[:, k, :],
                    in0=dead[:, K * b : K * (b + 1)],
                    scalar=pa[:, col : col + 1],
                    in1=sp[:],
                    op0=ALU.mult,
                    op1=ALU.subtract,
                )
                if last:
                    nc.vector.tensor_reduce(out=nm[:, k : k + 1], in_=z[:, k, :], axis=AX.X, op=ALU.min)
            if not last:
                nc.vector.tensor_reduce(out=nm[:], in_=z[:], axis=AX.X, op=ALU.min)
            for k in range(4):
                nc.scalar.activation(
                    out=z[:, k, :],
                    in_=z[:, k, :],
                    func=ACT.Exp,
                    bias=nm[:, k : k + 1],
                    scale=-1.0,
                    accum_out=ssum[:, k : k + 1],
                )
            rows = out[b].rearrange("(p t) j -> p t j", t=8)
            if last:
                for k in range(4):
                    nc.vector.reciprocal(out=r[:, k : k + 1], in_=ssum[:, k : k + 1])
                    nc.vector.tensor_scalar(
                        out=z[:, k, :], in0=z[:, k, :], scalar1=r[:, k : k + 1], scalar2=None, op0=ALU.mult
                    )
                    nc.sync.dma_start(out=rows[:, 4 * h + k, :], in_=z[:, k, :])
            else:
                nc.vector.reciprocal(out=r[:], in_=ssum[:])
                for k in range(4):
                    nc.gpsimd.tensor_scalar(
                        out=z[:, k, :],
                        in0=z[:, k, :],
                        scalar1=r[:, k : k + 1],
                        scalar2=0.0,
                        op0=ALU.mult,
                        op1=ALU.add,
                    )
                nc.sync.dma_start(out=rows[:, 4 * h : 4 * h + 4, :], in_=z[:])

        for n in range(UNITS + 2):
            if n < UNITS:
                b, h = n // 2, n % 2
                if h == 0:
                    if b + 2 < B:
                        load(b + 2)
                    stage_ctx(b)
                stage_x(n)
            if 1 <= n <= UNITS:
                stage_q(n - 1)
            if n >= 2:
                stage_s(n - 2)
